import numpy as np
import ml_dtypes


def mxq(x, axis, fmt="e4m3"):
    dtype, down = {"e4m3": (ml_dtypes.float8_e4m3fn, 7), "e5m2": (ml_dtypes.float8_e5m2, 14)}[fmt]
    v = np.moveaxis(np.asarray(x, np.float32).astype(ml_dtypes.bfloat16).astype(np.float64), axis, -1)
    blocks = v.reshape(v.shape[:-1] + (-1, 32))
    amax = np.abs(blocks).max(-1, keepdims=True)
    byte = np.maximum(np.where(amax > 0, np.frexp(amax)[1] - 1 + 127, 0) - down, 1)
    scale = np.exp2(byte - 127.0)
    codes = (blocks / scale).astype(np.float32).astype(dtype).astype(np.float64)
    return np.moveaxis((codes * scale).reshape(v.shape), -1, axis)


WIDE = False


def mx_kscale(k):
    if not WIDE:
        return np.ones(k)
    levels = np.array([30, -30])
    if k % 512:
        return np.exp2(np.random.permutation(np.resize(levels, k // 32))).repeat(32)
    a = np.empty((k // 512, 16))
    for p in range(k // 512):
        a[p, :8] = np.random.permutation(np.resize(levels, 8))
        for g in range(8):
            far = levels[np.abs(levels - a[p, g]) >= 10]
            a[p, g + 8] = far[np.random.randint(len(far))]
    return np.exp2(a.ravel()).repeat(32)


BF16 = ml_dtypes.bfloat16


def bf(x):
    return np.asarray(x, np.float32).astype(BF16)


def f64(x):
    return np.asarray(x).astype(np.float64)


B, C, T, E, H = 1, 512, 4, 1024, 8
D = E // H
S = C * T


def heads(y):
    return np.moveaxis(y.reshape(B, C, T, H, D), 3, 1)


def setup_inputs():
    s = mx_kscale(E)
    return {"hidden_states": bf(np.random.standard_normal((B, S, E)) * s),
            "wk": bf(np.random.standard_normal((E, E)) * 2.0 / np.sqrt(E) / s[None, :]),
            "bk": bf(np.random.standard_normal(E) * 0.3),
            "wv": bf(np.random.standard_normal((E, E)) * 2.0 / np.sqrt(E) / s[None, :]),
            "bv": bf(np.random.standard_normal(E) * 0.3)}


def reference(hidden_states, wk, bk, wv, bv):
    xq = mxq(f64(hidden_states), 2, "e5m2")
    k = heads((xq @ mxq(f64(wk), 1, "e5m2").T) + f64(bk))
    v = heads((xq @ mxq(f64(wv), 1, "e5m2").T) + f64(bv))
    return k, v, k.mean(axis=3), v.mean(axis=3)

@@ -1,0 +1,247 @@
+from contextlib import ExitStack
+
+import concourse.mybir as mybir
+from concourse.masks import make_identity
+
+FLOPS = 2 * 2048 * 1024 * 2048
+
+F32 = mybir.dt.float32
+BF16 = mybir.dt.bfloat16
+U32 = mybir.dt.uint32
+U8 = mybir.dt.uint8
+FP8X4 = mybir.dt.float8_e5m2_x4
+ADD = mybir.AluOpType.add
+MULT = mybir.AluOpType.mult
+COPY = mybir.ActivationFunctionType.Copy
+
+P = 128
+E = 1024
+NG = 4
+NT = 4
+NB = 4
+HB = 4
+D = 128
+
+VMODE = ((1, 3), (2, 3), (3, 3))
+SPLIT_BLOCK = 3
+FLUSH_LAG = 2
+FLUSH_GUARD = 6
+
+
+def tile_chunkedattention_pb_kernel(tc, hidden_states, wk, bk, wv, bv, out_0, out_1, out_2, out_3):
+    nc = tc.nc
+
+    x_view = hidden_states.flatten_outer_dims().rearrange("(p g t) k -> p g t k", g=NG, t=NT)
+    w_views = []
+    for n in range(NB):
+        w = (wk, wv)[n // 2]
+        w_views.append(w[512 * (n % 2) : 512 * (n % 2 + 1), :].rearrange("(j p) k -> p j k", p=P))
+    y_views = [o.rearrange("b h (p g) t d -> p g (b h) (t d)", g=NG) for o in (out_0, out_1)]
+    m_views = [o.rearrange("b h (p g) d -> p (b h) (g d)", g=NG) for o in (out_2, out_3)]
+
+    with ExitStack() as ctx:
+        const = ctx.enter_context(tc.tile_pool(name="const", bufs=1))
+        rawp = ctx.enter_context(tc.tile_pool(name="rawp", bufs=1))
+        codes = ctx.enter_context(tc.tile_pool(name="codes", bufs=1))
+        stage = ctx.enter_context(tc.tile_pool(name="stage", bufs=3))
+        ypool = ctx.enter_context(tc.tile_pool(name="ypool", bufs=6))
+        spool = ctx.enter_context(tc.tile_pool(name="spool", bufs=2))
+        mpool = ctx.enter_context(tc.tile_pool(name="mpool", bufs=2))
+        tpsum = ctx.enter_context(tc.psum_pool(name="tpsum", bufs=4))
+        apsum = ctx.enter_context(tc.psum_pool(name="apsum", bufs=4))
+        ctx.enter_context(tc.manual_schedule())
+
+        ones = const.tile([P, P], BF16, name="ones")
+        nc.vector.memset(ones[:], 1.0)
+        bias_rows = const.tile([P, 2 * E], BF16, name="bias_rows")
+        nc.vector.memset(bias_rows[:], 0.0)
+        warm = const.tile([P, 1], F32, name="warm")
+        nc.scalar.activation(out=warm[:], in_=ones[:, 0:1], func=COPY, scale=0.25)
+        ident = const.tile([P, P], F32, name="ident")
+        make_identity(nc, ident[:])
+        bias = const.tile([P, 2 * E], F32, name="bias")
+
+        units = (("w", 0), ("x", 0), ("x", 1), ("x", 2), ("x", 3), ("w", 1), ("w", 2), ("w", 3))
+        pieces = {("w", 0): 4, ("x", 0): 4, ("x", 1): 2}
+        raw = {}
+        for unit in units:
+            src = w_views[unit[1]] if unit[0] == "w" else x_view[:, unit[1], :, :]
+            rt = rawp.tile([P, 4, E], BF16, name="raw_%s%d" % unit)
+            raw[unit] = rt
+            n_dma = pieces.get(unit, 1)
+            step = 4 // n_dma
+            for i in range(n_dma):
+                nc.sync.dma_start(out=rt[:, i * step : (i + 1) * step, :], in_=src[:, i * step : (i + 1) * step, :])
+            if unit == ("w", 0):
+                nc.sync.dma_start(out=bias_rows[0:1, 0:E], in_=bk.rearrange("(o f) -> o f", o=1))
+                nc.sync.dma_start(out=bias_rows[0:1, E : 2 * E], in_=bv.rearrange("(o f) -> o f", o=1))
+
+        def bias_block(n):
+            bp = apsum.tile([P, 512], F32, name="acc")
+            nc.tensor.matmul(out=bp[:], lhsT=ones[:], rhs=bias_rows[:, 512 * n : 512 * (n + 1)], start=True, stop=True)
+            if n == 0:
+                nc.vector.tensor_copy(out=bias[:, 512 * n : 512 * (n + 1)], in_=bp[:])
+            else:
+                nc.scalar.copy(out=bias[:, 512 * n : 512 * (n + 1)], in_=bp[:])
+
+        xc = {}
+        xs = {}
+        wc = {}
+        ws = {}
+
+        def transpose_unit(unit):
+            kind, idx = unit
+            grp = stage.tile([P, 4096], BF16, name="grp", align_bytes=64)
+            gwords = grp[:].bitcast(F32)
+            if kind == "w":
+                for c in range(2):
+                    wc[(idx, c)] = codes.tile([P, 512], U32, name="wc%d_%d" % (idx, c), align_bytes=64)
+                    ws[(idx, c)] = codes.tile([P, 512], U8, name="ws%d_%d" % (idx, c), align_bytes=64)
+            else:
+                for h in range(2):
+                    xc[(idx, h)] = codes.tile([P, 512], U32, name="xc%d_%d" % (idx, h), align_bytes=64)
+                    xs[(idx, h)] = codes.tile([P, 512], U8, name="xs%d_%d" % (idx, h), align_bytes=64)
+            for s in range(4):
+                words = raw[unit][:, s, :].bitcast(F32)
+                tp = tpsum.tile([P, 4, P], F32, name="tp")
+                for c in range(2):
+                    for u in range(2):
+                        nc.tensor.transpose(tp[:, 2 * c + u, :], words[:, 256 * c + u : 256 * (c + 1) : 2], ident[:])
+                if kind == "w":
+                    dst = gwords.rearrange("p (c f u) -> p c f u", c=2, u=2)[:, :, P * s : P * (s + 1), :]
+                else:
+                    dst = gwords[:, 512 * s : 512 * (s + 1)].rearrange("p (c r u) -> p c r u", c=2, u=2)
+                nc.scalar.copy(out=dst, in_=tp[:].rearrange("p (c u) r -> p c r u", c=2))
+                if s % 2 == 1:
+                    h = s // 2
+                    if kind == "w":
+                        for c in range(2):
+                            lo = 2048 * c + 1024 * h
+                            nc.vector.quantize_mx(
+                                out=wc[(idx, c)][:, 256 * h : 256 * (h + 1)].bitcast(FP8X4),
+                                scales=ws[(idx, c)][:, 256 * h : 256 * (h + 1)],
+                                in_=grp[:, lo : lo + 1024],
+                            )
+                    else:
+                        nc.vector.quantize_mx(
+                            out=xc[(idx, h)][:].bitcast(FP8X4),
+                            scales=xs[(idx, h)][:],
+                            in_=grp[:, 2048 * h : 2048 * (h + 1)],
+                        )
+
+        state = {"y": None, "chain": None, "u": None, "seq": 0, "banks": 0, "late": False}
+        means = {}
+        parts = {}
+        pending_scales = []
+
+        def part_done(n, g):
+            parts.setdefault(n, []).append(g)
+            m = means[n]
+            dst = m_views[n // 2][:, HB * (n % 2) : HB * (n % 2 + 1), :]
+            if n == SPLIT_BLOCK:
+                half = g // 2
+                if (2 * half in parts[n]) and (2 * half + 1 in parts[n]):
+                    nc.scalar.dma_start(
+                        out=dst[:, :, 256 * half : 256 * (half + 1)],
+                        in_=m[:, :, 2 * half : 2 * half + 2, :].rearrange("p h g d -> p h (g d)"),
+                    )
+            elif len(parts[n]) == NG:
+                nc.scalar.dma_start(out=dst, in_=m[:].rearrange("p h g d -> p h (g d)"))
+
+        def flush_scales(upto):
+            for item in list(pending_scales):
+                r, n, g, seq = item
+                if seq <= upto:
+                    nc.scalar.activation(
+                        out=means[n][:, :, g, :], in_=r[:].rearrange("p (h d) -> p h d", h=HB), func=COPY, scale=0.25
+                    )
+                    pending_scales.remove(item)
+                    part_done(n, g)
+
+        def bank(n, g, t):
+            if n not in means:
+                means[n] = mpool.tile([P, HB, NG, D], F32, name="means")
+            if t == 0:
+                state["y"] = ypool.tile([P, HB, NT, D], F32, name="y")
+            y = state["y"]
+            m = means[n]
+            state["banks"] += 1
+            if state["late"] and state["banks"] % 2 == 1:
+                acc = tpsum.tile([P, 512], F32, name="tp")
+            else:
+                acc = apsum.tile([P, 512], F32, name="acc")
+            for c in range(2):
+                lo = 256 * (t % 2) + P * c
+                nc.tensor.matmul_mx(
+                    out=acc[:],
+                    lhsT=xc[(g, t // 2)][:, lo : lo + P].bitcast(FP8X4),
+                    lhsT_scale=xs[(g, t // 2)][:, lo : lo + P],
+                    rhs=wc[(n, c)][:].bitcast(FP8X4),
+                    rhs_scale=ws[(n, c)][:],
+                    start=(c == 0),
+                    stop=(c == 1),
+                )
+            b_n = bias[:, 512 * n : 512 * (n + 1)]
+            acc3 = acc[:].rearrange("p (h d) -> p h d", h=HB)
+            nc.vector.tensor_tensor(out=y[:, :, t, :], in0=acc3, in1=b_n.rearrange("p (h d) -> p h d", h=HB), op=ADD)
+            y_dst = y_views[n // 2][:, g, HB * (n % 2) : HB * (n % 2 + 1), :]
+            last_unit = n == NB - 1 and g == NG - 1
+            if last_unit and t % 2 == 1:
+                nc.sync.dma_start(
+                    out=y_dst[:, :, D * (t - 1) : D * (t + 1)],
+                    in_=y[:, :, t - 1 : t + 1, :].rearrange("p h t d -> p h (t d)"),
+                )
+            elif t == NT - 1:
+                nc.sync.dma_start(out=y_dst, in_=y[:].rearrange("p h t d -> p h (t d)"))
+            if (n, g) in VMODE:
+                prev = b_n if t == 0 else state["chain"][:]
+                if t < NT - 1:
+                    ch = spool.tile([P, 512], F32, name="chain")
+                    nc.vector.scalar_tensor_tensor(out=ch[:], in0=acc[:], scalar=0.25, in1=prev, op0=MULT, op1=ADD)
+                    state["chain"] = ch
+                else:
+                    nc.vector.scalar_tensor_tensor(
+                        out=m[:, :, g, :], in0=acc3, scalar=0.25, in1=prev.rearrange("p (h d) -> p h d", h=HB), op0=MULT, op1=ADD
+                    )
+                    part_done(n, g)
+            else:
+                if t == 1:
+                    u = spool.tile([P, HB, D], F32, name="pair_a")
+                    nc.gpsimd.tensor_tensor(out=u[:], in0=y[:, :, 0, :], in1=y[:, :, 1, :], op=ADD)
+                    state["u"] = u
+                if t == 3:
+                    w2 = spool.tile([P, HB, D], F32, name="pair_b")
+                    nc.gpsimd.tensor_tensor(out=w2[:], in0=y[:, :, 2, :], in1=y[:, :, 3, :], op=ADD)
+                    r = spool.tile([P, 512], F32, name="total", bufs=5)
+                    nc.gpsimd.tensor_tensor(
+                        out=r[:].rearrange("p (h d) -> p h d", h=HB), in0=state["u"][:], in1=w2[:], op=ADD
+                    )
+                    pending_scales.append((r, n, g, state["seq"]))
+
+        banks = [(n, g, t) for n in range(NB) for g in range(NG) for t in range(NT)]
+        program = (
+            ("T", ("w", 0)), ("B", 0), ("T", ("x", 0)), ("M", 2), ("B", 1), ("T", ("x", 1)), ("M", 4),
+            ("B", 2), ("T", ("x", 2)), ("M", 4), ("B", 3), ("T", ("x", 3)), ("M", 4),
+            ("T", ("w", 1)), ("M", 16), ("T", ("w", 2)), ("M", 16), ("T", ("w", 3)), ("M", 18),
+        )
+        pos = 0
+        for kind, arg in program:
+            if kind == "T":
+                transpose_unit(arg)
+                flush_scales(state["seq"])
+                if arg == ("w", 3):
+                    state["late"] = True
+            elif kind == "B":
+                bias_block(arg)
+            else:
+                for i in range(arg):
+                    b = banks[pos + i]
+                    bank(b[0], b[1], b[2])
+                    if b[2] == NT - 1:
+                        if state["late"]:
+                            flush_scales(state["seq"])
+                        elif arg - 1 - i >= FLUSH_GUARD:
+                            flush_scales(state["seq"] - FLUSH_LAG)
+                        state["seq"] += 1
+                pos += arg
+        flush_scales(state["seq"])

@@ -22,7 +22,7 @@ NB = 4
 HB = 4
 D = 128
 
-VMODE = ((1, 3), (2, 3), (3, 3))
+VMODE = ((0, 0), (0, 1), (1, 3), (2, 3), (3, 3))
 SPLIT_BLOCK = 3
 FLUSH_LAG = 2
 FLUSH_GUARD = 6
@@ -53,6 +53,8 @@ def tile_chunkedattention_pb_kernel(tc, hidden_states, wk, bk, wv, bv, out_0, ou
 
         ones = const.tile([P, P], BF16, name="ones")
         nc.vector.memset(ones[:], 1.0)
+        dummy_rhs = const.tile([P, 512], BF16, name="dummy_rhs")
+        nc.vector.memset(dummy_rhs[:], 1.0)
         bias_rows = const.tile([P, 2 * E], BF16, name="bias_rows")
         nc.vector.memset(bias_rows[:], 0.0)
         warm = const.tile([P, 1], F32, name="warm")
@@ -60,6 +62,13 @@ def tile_chunkedattention_pb_kernel(tc, hidden_states, wk, bk, wv, bv, out_0, ou
         ident = const.tile([P, P], F32, name="ident")
         make_identity(nc, ident[:])
         bias = const.tile([P, 2 * E], F32, name="bias")
+        dummy_out = apsum.tile([P, 512], F32, name="acc")
+
+        def dummy_matmul():
+            nc.tensor.matmul(out=dummy_out[:], lhsT=ones[:], rhs=dummy_rhs[:], start=True, stop=True)
+
+        for i in range(4):
+            dummy_matmul()
 
         units = (("w", 0), ("x", 0), ("x", 1), ("x", 2), ("x", 3), ("w", 1), ("w", 2), ("w", 3))
         pieces = {("w", 0): 4, ("x", 0): 4, ("x", 1): 2}
@@ -79,10 +88,7 @@ def tile_chunkedattention_pb_kernel(tc, hidden_states, wk, bk, wv, bv, out_0, ou
         def bias_block(n):
             bp = apsum.tile([P, 512], F32, name="acc")
             nc.tensor.matmul(out=bp[:], lhsT=ones[:], rhs=bias_rows[:, 512 * n : 512 * (n + 1)], start=True, stop=True)
-            if n == 0:
-                nc.vector.tensor_copy(out=bias[:, 512 * n : 512 * (n + 1)], in_=bp[:])
-            else:
-                nc.scalar.copy(out=bias[:, 512 * n : 512 * (n + 1)], in_=bp[:])
+            nc.scalar.copy(out=bias[:, 512 * n : 512 * (n + 1)], in_=bp[:])
 
         xc = {}
         xs = {}
@@ -107,6 +113,8 @@ def tile_chunkedattention_pb_kernel(tc, hidden_states, wk, bk, wv, bv, out_0, ou
                 for c in range(2):
                     for u in range(2):
                         nc.tensor.transpose(tp[:, 2 * c + u, :], words[:, 256 * c + u : 256 * (c + 1) : 2], ident[:])
+                if unit in (("w", 0), ("x", 0)):
+                    dummy_matmul()
                 if kind == "w":
                     dst = gwords.rearrange("p (c f u) -> p c f u", c=2, u=2)[:, :, P * s : P * (s + 1), :]
                 else:
@@ -220,9 +228,9 @@ def tile_chunkedattention_pb_kernel(tc, hidden_states, wk, bk, wv, bv, out_0, ou
 
         banks = [(n, g, t) for n in range(NB) for g in range(NG) for t in range(NT)]
         program = (
-            ("T", ("w", 0)), ("B", 0), ("T", ("x", 0)), ("M", 2), ("B", 1), ("T", ("x", 1)), ("M", 4),
-            ("B", 2), ("T", ("x", 2)), ("M", 4), ("B", 3), ("T", ("x", 3)), ("M", 4),
-            ("T", ("w", 1)), ("M", 16), ("T", ("w", 2)), ("M", 16), ("T", ("w", 3)), ("M", 18),
+            ("T", ("w", 0)), ("B", 0), ("T", ("x", 0)), ("M", 2), ("B", 1), ("T", ("x", 1)), ("M", 2),
+            ("B", 2), ("T", ("x", 2)), ("M", 2), ("B", 3), ("T", ("x", 3)), ("M", 2),
+            ("T", ("w", 1)), ("M", 2), ("T", ("w", 2)), ("M", 2), ("T", ("w", 3)), ("M", 52),
         )
         pos = 0
         for kind, arg in program:

@@ -22,7 +22,7 @@ NB = 4
 HB = 4
 D = 128
 
-VMODE = ((0, 0), (0, 1), (1, 3), (2, 3), (3, 3))
+VMODE = ((0, 0), (0, 1), (1, 1), (2, 2), (3, 2), (3, 3))
 SPLIT_BLOCK = 3
 FLUSH_LAG = 2
 FLUSH_GUARD = 6
@@ -137,7 +137,7 @@ def tile_chunkedattention_pb_kernel(tc, hidden_states, wk, bk, wv, bv, out_0, ou
                             in_=grp[:, 2048 * h : 2048 * (h + 1)],
                         )
 
-        state = {"y": None, "chain": None, "u": None, "seq": 0, "banks": 0, "late": False}
+        state = {"y": None, "chain": None, "seq": 0, "banks": 0, "late": False}
         means = {}
         parts = {}
         pending_scales = []
@@ -147,12 +147,10 @@ def tile_chunkedattention_pb_kernel(tc, hidden_states, wk, bk, wv, bv, out_0, ou
             m = means[n]
             dst = m_views[n // 2][:, HB * (n % 2) : HB * (n % 2 + 1), :]
             if n == SPLIT_BLOCK:
-                half = g // 2
-                if (2 * half in parts[n]) and (2 * half + 1 in parts[n]):
-                    nc.scalar.dma_start(
-                        out=dst[:, :, 256 * half : 256 * (half + 1)],
-                        in_=m[:, :, 2 * half : 2 * half + 2, :].rearrange("p h g d -> p h (g d)"),
-                    )
+                if g >= 2:
+                    nc.scalar.dma_start(out=dst[:, :, D * g : D * (g + 1)], in_=m[:, :, g, :])
+                elif (0 in parts[n]) and (1 in parts[n]):
+                    nc.scalar.dma_start(out=dst[:, :, 0 : 2 * D], in_=m[:, :, 0:2, :].rearrange("p h g d -> p h (g d)"))
             elif len(parts[n]) == NG:
                 nc.scalar.dma_start(out=dst, in_=m[:].rearrange("p h g d -> p h (g d)"))
 
@@ -194,11 +192,11 @@ def tile_chunkedattention_pb_kernel(tc, hidden_states, wk, bk, wv, bv, out_0, ou
             nc.vector.tensor_tensor(out=y[:, :, t, :], in0=acc3, in1=b_n.rearrange("p (h d) -> p h d", h=HB), op=ADD)
             y_dst = y_views[n // 2][:, g, HB * (n % 2) : HB * (n % 2 + 1), :]
             last_unit = n == NB - 1 and g == NG - 1
-            if last_unit and t % 2 == 1:
-                nc.sync.dma_start(
-                    out=y_dst[:, :, D * (t - 1) : D * (t + 1)],
-                    in_=y[:, :, t - 1 : t + 1, :].rearrange("p h t d -> p h (t d)"),
-                )
+            if last_unit:
+                if t == 1:
+                    nc.sync.dma_start(out=y_dst[:, :, 0 : 2 * D], in_=y[:, :, 0:2, :].rearrange("p h t d -> p h (t d)"))
+                elif t >= 2:
+                    nc.sync.dma_start(out=y_dst[:, :, D * t : D * (t + 1)], in_=y[:, :, t, :])
             elif t == NT - 1:
                 nc.sync.dma_start(out=y_dst, in_=y[:].rearrange("p h t d -> p h (t d)"))
             if (n, g) in VMODE:
@@ -213,16 +211,12 @@ def tile_chunkedattention_pb_kernel(tc, hidden_states, wk, bk, wv, bv, out_0, ou
                     )
                     part_done(n, g)
             else:
-                if t == 1:
-                    u = spool.tile([P, HB, D], F32, name="pair_a")
-                    nc.gpsimd.tensor_tensor(out=u[:], in0=y[:, :, 0, :], in1=y[:, :, 1, :], op=ADD)
-                    state["u"] = u
                 if t == 3:
-                    w2 = spool.tile([P, HB, D], F32, name="pair_b")
-                    nc.gpsimd.tensor_tensor(out=w2[:], in0=y[:, :, 2, :], in1=y[:, :, 3, :], op=ADD)
+                    pairs = spool.tile([P, HB, 2, D], F32, name="pairs")
+                    nc.gpsimd.tensor_tensor(out=pairs[:], in0=y[:, :, 0:4:2, :], in1=y[:, :, 1:4:2, :], op=ADD)
                     r = spool.tile([P, 512], F32, name="total", bufs=5)
                     nc.gpsimd.tensor_tensor(
-                        out=r[:].rearrange("p (h d) -> p h d", h=HB), in0=state["u"][:], in1=w2[:], op=ADD
+                        out=r[:].rearrange("p (h d) -> p h d", h=HB), in0=pairs[:, :, 0, :], in1=pairs[:, :, 1, :], op=ADD
                     )
                     pending_scales.append((r, n, g, state["seq"]))
 

@@ -22,7 +22,7 @@ NB = 4
 HB = 4
 D = 128
 
-VMODE = ((0, 0), (0, 1), (1, 1), (2, 2), (3, 2), (3, 3))
+VMODE = ((0, 0), (0, 1), (0, 2), (1, 2), (2, 3), (3, 3))
 SPLIT_BLOCK = 3
 FLUSH_LAG = 2
 FLUSH_GUARD = 6
@@ -95,19 +95,23 @@ def tile_chunkedattention_pb_kernel(tc, hidden_states, wk, bk, wv, bv, out_0, ou
         wc = {}
         ws = {}
 
-        def transpose_unit(unit):
+        grps = {}
+
+        def transpose_unit(unit, first, last):
             kind, idx = unit
-            grp = stage.tile([P, 4096], BF16, name="grp", align_bytes=64)
+            if first == 0:
+                grps[unit] = stage.tile([P, 4096], BF16, name="grp", align_bytes=64)
+                if kind == "w":
+                    for c in range(2):
+                        wc[(idx, c)] = codes.tile([P, 512], U32, name="wc%d_%d" % (idx, c), align_bytes=64)
+                        ws[(idx, c)] = codes.tile([P, 512], U8, name="ws%d_%d" % (idx, c), align_bytes=64)
+                else:
+                    for h in range(2):
+                        xc[(idx, h)] = codes.tile([P, 512], U32, name="xc%d_%d" % (idx, h), align_bytes=64)
+                        xs[(idx, h)] = codes.tile([P, 512], U8, name="xs%d_%d" % (idx, h), align_bytes=64)
+            grp = grps[unit]
             gwords = grp[:].bitcast(F32)
-            if kind == "w":
-                for c in range(2):
-                    wc[(idx, c)] = codes.tile([P, 512], U32, name="wc%d_%d" % (idx, c), align_bytes=64)
-                    ws[(idx, c)] = codes.tile([P, 512], U8, name="ws%d_%d" % (idx, c), align_bytes=64)
-            else:
-                for h in range(2):
-                    xc[(idx, h)] = codes.tile([P, 512], U32, name="xc%d_%d" % (idx, h), align_bytes=64)
-                    xs[(idx, h)] = codes.tile([P, 512], U8, name="xs%d_%d" % (idx, h), align_bytes=64)
-            for s in range(4):
+            for s in range(first, last):
                 words = raw[unit][:, s, :].bitcast(F32)
                 tp = tpsum.tile([P, 4, P], F32, name="tp")
                 for c in range(2):
@@ -137,7 +141,7 @@ def tile_chunkedattention_pb_kernel(tc, hidden_states, wk, bk, wv, bv, out_0, ou
                             in_=grp[:, 2048 * h : 2048 * (h + 1)],
                         )
 
-        state = {"y": None, "chain": None, "seq": 0, "banks": 0, "late": False}
+        state = {"y": None, "chain": None, "u": None, "seq": 0, "banks": 0, "late": False}
         means = {}
         parts = {}
         pending_scales = []
@@ -211,27 +215,36 @@ def tile_chunkedattention_pb_kernel(tc, hidden_states, wk, bk, wv, bv, out_0, ou
                     )
                     part_done(n, g)
             else:
+                if t == 1:
+                    u = spool.tile([P, HB, D], F32, name="pair_a")
+                    nc.gpsimd.tensor_tensor(out=u[:], in0=y[:, :, 0, :], in1=y[:, :, 1, :], op=ADD)
+                    state["u"] = u
                 if t == 3:
-                    pairs = spool.tile([P, HB, 2, D], F32, name="pairs")
-                    nc.gpsimd.tensor_tensor(out=pairs[:], in0=y[:, :, 0:4:2, :], in1=y[:, :, 1:4:2, :], op=ADD)
+                    w2 = spool.tile([P, HB, D], F32, name="pair_b")
+                    nc.gpsimd.tensor_tensor(out=w2[:], in0=y[:, :, 2, :], in1=y[:, :, 3, :], op=ADD)
                     r = spool.tile([P, 512], F32, name="total", bufs=5)
                     nc.gpsimd.tensor_tensor(
-                        out=r[:].rearrange("p (h d) -> p h d", h=HB), in0=pairs[:, :, 0, :], in1=pairs[:, :, 1, :], op=ADD
+                        out=r[:].rearrange("p (h d) -> p h d", h=HB), in0=state["u"][:], in1=w2[:], op=ADD
                     )
                     pending_scales.append((r, n, g, state["seq"]))
 
         banks = [(n, g, t) for n in range(NB) for g in range(NG) for t in range(NT)]
-        program = (
-            ("T", ("w", 0)), ("B", 0), ("T", ("x", 0)), ("M", 2), ("B", 1), ("T", ("x", 1)), ("M", 2),
-            ("B", 2), ("T", ("x", 2)), ("M", 2), ("B", 3), ("T", ("x", 3)), ("M", 2),
-            ("T", ("w", 1)), ("M", 2), ("T", ("w", 2)), ("M", 2), ("T", ("w", 3)), ("M", 52),
-        )
+        program = [("T", ("w", 0, 0, 4)), ("B", 0), ("T", ("x", 0, 0, 4))]
+        later = (("x", 1), ("x", 2), ("x", 3), ("w", 1), ("w", 2), ("w", 3))
+        for i in range(len(later)):
+            program.append(("M", 1))
+            if i < 3:
+                program.append(("B", i + 1))
+            program.append(("T", (later[i][0], later[i][1], 0, 2)))
+            program.append(("M", 1))
+            program.append(("T", (later[i][0], later[i][1], 2, 4)))
+        program.append(("M", 52))
         pos = 0
         for kind, arg in program:
             if kind == "T":
-                transpose_unit(arg)
+                transpose_unit((arg[0], arg[1]), arg[2], arg[3])
                 flush_scales(state["seq"])
-                if arg == ("w", 3):
+                if arg == ("w", 3, 2, 4):
                     state["late"] = True
             elif kind == "B":
                 bias_block(arg)

@@ -22,7 +22,10 @@ NB = 4
 HB = 4
 D = 128
 
-VMODE = ((0, 0), (0, 1), (0, 2), (1, 2), (2, 3), (3, 3))
+VMODE = ((0, 0), (0, 1), (0, 2), (3, 3))
+TMODE = ((1, 0), (1, 3), (2, 2), (3, 0))
+T_ACC_LAG = 8
+T_BACK_LAG = 11
 SPLIT_BLOCK = 3
 FLUSH_LAG = 2
 FLUSH_GUARD = 6
@@ -145,6 +148,36 @@ def tile_chunkedattention_pb_kernel(tc, hidden_states, wk, bk, wv, bv, out_0, ou
         means = {}
         parts = {}
         pending_scales = []
+        t_acc_wait = []
+        t_back_wait = []
+
+        def t_accumulate(y, n, g):
+            at = tpsum.tile([P, HB, P], F32, name="tp")
+            for h in range(HB):
+                for t in range(NT):
+                    nc.tensor.matmul(
+                        out=at[:, h, :], lhsT=y[:, h, t, :], rhs=ident[:], is_transpose=True, start=(t == 0), stop=(t == NT - 1)
+                    )
+            mt = spool.tile([P, HB, P], F32, name="mean_t")
+            nc.scalar.activation(out=mt[:], in_=at[:], func=COPY, scale=0.25)
+            return mt
+
+        def t_back(mt, n, g):
+            bt = tpsum.tile([P, HB, P], F32, name="tp")
+            for h in range(HB):
+                nc.tensor.transpose(bt[:, h, :], mt[:, h, :], ident[:])
+            nc.scalar.copy(out=means[n][:, :, g, :], in_=bt[:])
+            part_done(n, g)
+
+        def t_steps(k):
+            for item in list(t_back_wait):
+                if k >= item[3] + T_BACK_LAG:
+                    t_back(item[0], item[1], item[2])
+                    t_back_wait.remove(item)
+            for item in list(t_acc_wait):
+                if k >= item[3] + T_ACC_LAG:
+                    t_back_wait.append((t_accumulate(item[0], item[1], item[2]), item[1], item[2], item[3]))
+                    t_acc_wait.remove(item)
 
         def part_done(n, g):
             parts.setdefault(n, []).append(g)
@@ -214,6 +247,9 @@ def tile_chunkedattention_pb_kernel(tc, hidden_states, wk, bk, wv, bv, out_0, ou
                         out=m[:, :, g, :], in0=acc3, scalar=0.25, in1=prev.rearrange("p (h d) -> p h d", h=HB), op0=MULT, op1=ADD
                     )
                     part_done(n, g)
+            elif (n, g) in TMODE:
+                if t == NT - 1:
+                    t_acc_wait.append((y, n, g, state["banks"] - 1))
             else:
                 if t == 1:
                     u = spool.tile([P, HB, D], F32, name="pair_a")
@@ -252,9 +288,10 @@ def tile_chunkedattention_pb_kernel(tc, hidden_states, wk, bk, wv, bv, out_0, ou
                 for i in range(arg):
                     b = banks[pos + i]
                     bank(b[0], b[1], b[2])
+                    t_steps(pos + i)
                     if b[2] == NT - 1:
                         if state["late"]:
-                            flush_scales(state["seq"])
+                            flush_scales(state["seq"] - FLUSH_LAG)
                         elif arg - 1 - i >= FLUSH_GUARD:
                             flush_scales(state["seq"] - FLUSH_LAG)
                         state["seq"] += 1

@@ -22,10 +22,11 @@ NB = 4
 HB = 4
 D = 128
 
-VMODE = ((0, 0), (0, 1), (0, 2), (3, 3))
-TMODE = ((1, 0), (1, 3), (2, 2), (3, 0))
+VMODE = ((0, 0), (0, 1), (0, 2), (2, 0), (3, 3))
+TMODE = ((1, 1), (2, 3))
 T_ACC_LAG = 8
 T_BACK_LAG = 11
+PAIR_FROM = 6
 SPLIT_BLOCK = 3
 FLUSH_LAG = 2
 FLUSH_GUARD = 6
@@ -40,14 +41,14 @@ def tile_chunkedattention_pb_kernel(tc, hidden_states, wk, bk, wv, bv, out_0, ou
         w = (wk, wv)[n // 2]
         w_views.append(w[512 * (n % 2) : 512 * (n % 2 + 1), :].rearrange("(j p) k -> p j k", p=P))
     y_views = [o.rearrange("b h (p g) t d -> p g (b h) (t d)", g=NG) for o in (out_0, out_1)]
+    pair_views = [o.rearrange("b h (p q e) t d -> p q (b h) (e t d)", q=NG // 2, e=2) for o in (out_0, out_1)]
     m_views = [o.rearrange("b h (p g) d -> p (b h) (g d)", g=NG) for o in (out_2, out_3)]
 
     with ExitStack() as ctx:
         const = ctx.enter_context(tc.tile_pool(name="const", bufs=1))
-        rawp = ctx.enter_context(tc.tile_pool(name="rawp", bufs=1))
+        big = ctx.enter_context(tc.tile_pool(name="big", bufs=7))
         codes = ctx.enter_context(tc.tile_pool(name="codes", bufs=1))
         stage = ctx.enter_context(tc.tile_pool(name="stage", bufs=3))
-        ypool = ctx.enter_context(tc.tile_pool(name="ypool", bufs=6))
         spool = ctx.enter_context(tc.tile_pool(name="spool", bufs=2))
         mpool = ctx.enter_context(tc.tile_pool(name="mpool", bufs=2))
         tpsum = ctx.enter_context(tc.psum_pool(name="tpsum", bufs=4))
@@ -76,14 +77,18 @@ def tile_chunkedattention_pb_kernel(tc, hidden_states, wk, bk, wv, bv, out_0, ou
         units = (("w", 0), ("x", 0), ("x", 1), ("x", 2), ("x", 3), ("w", 1), ("w", 2), ("w", 3))
         pieces = {("w", 0): 4, ("x", 0): 4, ("x", 1): 2}
         raw = {}
-        for unit in units:
+        for number, unit in enumerate(units):
             src = w_views[unit[1]] if unit[0] == "w" else x_view[:, unit[1], :, :]
-            rt = rawp.tile([P, 4, E], BF16, name="raw_%s%d" % unit)
-            raw[unit] = rt
+            if number % 2 == 0:
+                two_units = big.tile([P, 8, E], BF16, name="big")
+            base = 4 * (number % 2)
+            raw[unit] = (two_units, base)
             n_dma = pieces.get(unit, 1)
             step = 4 // n_dma
             for i in range(n_dma):
-                nc.sync.dma_start(out=rt[:, i * step : (i + 1) * step, :], in_=src[:, i * step : (i + 1) * step, :])
+                nc.sync.dma_start(
+                    out=two_units[:, base + i * step : base + (i + 1) * step, :], in_=src[:, i * step : (i + 1) * step, :]
+                )
             if unit == ("w", 0):
                 nc.sync.dma_start(out=bias_rows[0:1, 0:E], in_=bk.rearrange("(o f) -> o f", o=1))
                 nc.sync.dma_start(out=bias_rows[0:1, E : 2 * E], in_=bv.rearrange("(o f) -> o f", o=1))
@@ -115,7 +120,7 @@ def tile_chunkedattention_pb_kernel(tc, hidden_states, wk, bk, wv, bv, out_0, ou
             grp = grps[unit]
             gwords = grp[:].bitcast(F32)
             for s in range(first, last):
-                words = raw[unit][:, s, :].bitcast(F32)
+                words = raw[unit][0][:, raw[unit][1] + s, :].bitcast(F32)
                 tp = tpsum.tile([P, 4, P], F32, name="tp")
                 for c in range(2):
                     for u in range(2):
@@ -204,9 +209,10 @@ def tile_chunkedattention_pb_kernel(tc, hidden_states, wk, bk, wv, bv, out_0, ou
         def bank(n, g, t):
             if n not in means:
                 means[n] = mpool.tile([P, HB, NG, D], F32, name="means")
-            if t == 0:
-                state["y"] = ypool.tile([P, HB, NT, D], F32, name="y")
-            y = state["y"]
+            if t == 0 and g % 2 == 0:
+                state["pair"] = big.tile([P, HB, 2, NT, D], F32, name="big")
+            pair = state["pair"]
+            y = pair[:, :, g % 2, :, :]
             m = means[n]
             state["banks"] += 1
             if state["late"] and state["banks"] % 2 == 1:
@@ -229,13 +235,20 @@ def tile_chunkedattention_pb_kernel(tc, hidden_states, wk, bk, wv, bv, out_0, ou
             nc.vector.tensor_tensor(out=y[:, :, t, :], in0=acc3, in1=b_n.rearrange("p (h d) -> p h d", h=HB), op=ADD)
             y_dst = y_views[n // 2][:, g, HB * (n % 2) : HB * (n % 2 + 1), :]
             last_unit = n == NB - 1 and g == NG - 1
+            alone = (n == NB - 1 and g >= NG - 2) or NG * n + g < PAIR_FROM
             if last_unit:
                 if t == 1:
                     nc.sync.dma_start(out=y_dst[:, :, 0 : 2 * D], in_=y[:, :, 0:2, :].rearrange("p h t d -> p h (t d)"))
                 elif t >= 2:
                     nc.sync.dma_start(out=y_dst[:, :, D * t : D * (t + 1)], in_=y[:, :, t, :])
-            elif t == NT - 1:
-                nc.sync.dma_start(out=y_dst, in_=y[:].rearrange("p h t d -> p h (t d)"))
+            elif alone:
+                if t == NT - 1:
+                    nc.sync.dma_start(out=y_dst, in_=y.rearrange("p h t d -> p h (t d)"))
+            elif t == NT - 1 and g % 2 == 1:
+                nc.sync.dma_start(
+                    out=pair_views[n // 2][:, g // 2, HB * (n % 2) : HB * (n % 2 + 1), :],
+                    in_=pair[:].rearrange("p h e t d -> p h (e t d)"),
+                )
             if (n, g) in VMODE:
                 prev = b_n if t == 0 else state["chain"][:]
                 if t < NT - 1:

@@ -27,7 +27,7 @@ TMODE = ((1, 1), (2, 3))
 T_ACC_LAG = 8
 T_BACK_LAG = 11
 PAIR_FROM = 6
-SPLIT_BLOCK = 3
+SPLIT_BLOCK = 9
 FLUSH_LAG = 2
 FLUSH_GUARD = 6
 
@@ -234,7 +234,7 @@ def tile_chunkedattention_pb_kernel(tc, hidden_states, wk, bk, wv, bv, out_0, ou
             acc3 = acc[:].rearrange("p (h d) -> p h d", h=HB)
             nc.vector.tensor_tensor(out=y[:, :, t, :], in0=acc3, in1=b_n.rearrange("p (h d) -> p h d", h=HB), op=ADD)
             y_dst = y_views[n // 2][:, g, HB * (n % 2) : HB * (n % 2 + 1), :]
-            last_unit = n == NB - 1 and g == NG - 1
+            last_unit = False
             alone = (n == NB - 1 and g >= NG - 2) or NG * n + g < PAIR_FROM
             if last_unit:
                 if t == 1:

@@ -59,13 +59,14 @@ def tile_chunkedattention_pb_kernel(tc, hidden_states, wk, bk, wv, bv, out_0, ou
         nc.vector.memset(ones[:], 1.0)
         dummy_rhs = const.tile([P, 512], BF16, name="dummy_rhs")
         nc.vector.memset(dummy_rhs[:], 1.0)
-        bias_rows = const.tile([P, 2 * E], BF16, name="bias_rows")
+        bias_late = const.tile([P, 2 * E], BF16, name="bias_late")
+        bias_rows = const.tile([P, 512], BF16, name="bias_rows")
         nc.vector.memset(bias_rows[:], 0.0)
         warm = const.tile([P, 1], F32, name="warm")
         nc.scalar.activation(out=warm[:], in_=ones[:, 0:1], func=COPY, scale=0.25)
         ident = const.tile([P, P], F32, name="ident")
         make_identity(nc, ident[:])
-        bias = const.tile([P, 2 * E], F32, name="bias")
+        bias = const.tile([P, 512], F32, name="bias")
         dummy_out = apsum.tile([P, 512], F32, name="acc")
 
         def dummy_matmul():
@@ -90,8 +91,9 @@ def tile_chunkedattention_pb_kernel(tc, hidden_states, wk, bk, wv, bv, out_0, ou
                     out=two_units[:, base + i * step : base + (i + 1) * step, :], in_=src[:, i * step : (i + 1) * step, :]
                 )
             if unit == ("w", 0):
-                nc.sync.dma_start(out=bias_rows[0:1, 0:E], in_=bk.rearrange("(o f) -> o f", o=1))
-                nc.sync.dma_start(out=bias_rows[0:1, E : 2 * E], in_=bv.rearrange("(o f) -> o f", o=1))
+                nc.sync.dma_start(out=bias_rows[0:1, 0:512], in_=bk[0:512].rearrange("(o f) -> o f", o=1))
+        nc.sync.dma_start(out=bias_late[:, 512:E], in_=bk[512:E].partition_broadcast(P))
+        nc.sync.dma_start(out=bias_late[:, E : 2 * E], in_=bv.partition_broadcast(P))
 
         def bias_block(n):
             bp = apsum.tile([P, 512], F32, name="acc")
@@ -230,7 +232,7 @@ def tile_chunkedattention_pb_kernel(tc, hidden_states, wk, bk, wv, bv, out_0, ou
                     start=(c == 0),
                     stop=(c == 1),
                 )
-            b_n = bias[:, 512 * n : 512 * (n + 1)]
+            b_n = bias[:] if n == 0 else bias_late[:, 512 * n : 512 * (n + 1)]
             acc3 = acc[:].rearrange("p (h d) -> p h d", h=HB)
             nc.vector.tensor_tensor(out=y[:, :, t, :], in0=acc3, in1=b_n.rearrange("p (h d) -> p h d", h=HB), op=ADD)
             y_dst = y_views[n // 2][:, g, HB * (n % 2) : HB * (n % 2 + 1), :]
@@ -282,8 +284,6 @@ def tile_chunkedattention_pb_kernel(tc, hidden_states, wk, bk, wv, bv, out_0, ou
         later = (("x", 1), ("x", 2), ("x", 3), ("w", 1), ("w", 2), ("w", 3))
         for i in range(len(later)):
             program.append(("M", 1))
-            if i < 3:
-                program.append(("B", i + 1))
             program.append(("T", (later[i][0], later[i][1], 0, 2)))
             program.append(("M", 1))
             program.append(("T", (later[i][0], later[i][1], 2, 4)))

@@ -106,19 +106,20 @@ def tile_chunkedattention_pb_kernel(tc, hidden_states, wk, bk, wv, bv, out_0, ou
         ws = {}
 
         grps = {}
+        all_codes = {}
+        all_scales = {}
 
         def transpose_unit(unit, first, last):
             kind, idx = unit
             if first == 0:
                 grps[unit] = stage.tile([P, 4096], BF16, name="grp", align_bytes=64)
-                if kind == "w":
-                    for c in range(2):
-                        wc[(idx, c)] = codes.tile([P, 512], U32, name="wc%d_%d" % (idx, c), align_bytes=64)
-                        ws[(idx, c)] = codes.tile([P, 512], U8, name="ws%d_%d" % (idx, c), align_bytes=64)
-                else:
-                    for h in range(2):
-                        xc[(idx, h)] = codes.tile([P, 512], U32, name="xc%d_%d" % (idx, h), align_bytes=64)
-                        xs[(idx, h)] = codes.tile([P, 512], U8, name="xs%d_%d" % (idx, h), align_bytes=64)
+                all_codes[unit] = codes.tile([P, 1024], U32, name="codes_%s%d" % unit, align_bytes=64)
+                all_scales[unit] = codes.tile([P, 1024], U8, name="scales_%s%d" % unit, align_bytes=64)
+                code_views = wc if kind == "w" else xc
+                scale_views = ws if kind == "w" else xs
+                for half in range(2):
+                    code_views[(idx, half)] = all_codes[unit][:, 512 * half : 512 * (half + 1)]
+                    scale_views[(idx, half)] = all_scales[unit][:, 512 * half : 512 * (half + 1)]
             grp = grps[unit]
             gwords = grp[:].bitcast(F32)
             for s in range(first, last):
@@ -127,14 +128,18 @@ def tile_chunkedattention_pb_kernel(tc, hidden_states, wk, bk, wv, bv, out_0, ou
                 for c in range(2):
                     for u in range(2):
                         nc.tensor.transpose(tp[:, 2 * c + u, :], words[:, 256 * c + u : 256 * (c + 1) : 2], ident[:])
-                if unit in (("w", 0), ("x", 0)):
+                if unit in (("w", 0), ("x", 0)) and s % 2 == 1:
+                    dummy_matmul()
                     dummy_matmul()
                 if kind == "w":
                     dst = gwords.rearrange("p (c f u) -> p c f u", c=2, u=2)[:, :, P * s : P * (s + 1), :]
                 else:
                     dst = gwords[:, 512 * s : 512 * (s + 1)].rearrange("p (c r u) -> p c r u", c=2, u=2)
                 nc.scalar.copy(out=dst, in_=tp[:].rearrange("p (c u) r -> p c r u", c=2))
-                if s % 2 == 1:
+                if idx > 0:
+                    if s == 3:
+                        nc.vector.quantize_mx(out=all_codes[unit][:].bitcast(FP8X4), scales=all_scales[unit][:], in_=grp[:])
+                elif s % 2 == 1:
                     h = s // 2
                     if kind == "w":
                         for c in range(2):
@@ -146,8 +151,8 @@ def tile_chunkedattention_pb_kernel(tc, hidden_states, wk, bk, wv, bv, out_0, ou
                             )
                     else:
                         nc.vector.quantize_mx(
-                            out=xc[(idx, h)][:].bitcast(FP8X4),
-                            scales=xs[(idx, h)][:],
+                            out=xc[(idx, h)].bitcast(FP8X4),
+                            scales=xs[(idx, h)],
                             in_=grp[:, 2048 * h : 2048 * (h + 1)],
                         )
 
@@ -227,8 +232,8 @@ def tile_chunkedattention_pb_kernel(tc, hidden_states, wk, bk, wv, bv, out_0, ou
                     out=acc[:],
                     lhsT=xc[(g, t // 2)][:, lo : lo + P].bitcast(FP8X4),
                     lhsT_scale=xs[(g, t // 2)][:, lo : lo + P],
-                    rhs=wc[(n, c)][:].bitcast(FP8X4),
-                    rhs_scale=ws[(n, c)][:],
+                    rhs=wc[(n, c)].bitcast(FP8X4),
+                    rhs_scale=ws[(n, c)],
                     start=(c == 0),
                     stop=(c == 1),
                 )
@@ -237,7 +242,7 @@ def tile_chunkedattention_pb_kernel(tc, hidden_states, wk, bk, wv, bv, out_0, ou
             nc.vector.tensor_tensor(out=y[:, :, t, :], in0=acc3, in1=b_n.rearrange("p (h d) -> p h d", h=HB), op=ADD)
             y_dst = y_views[n // 2][:, g, HB * (n % 2) : HB * (n % 2 + 1), :]
             last_unit = False
-            alone = (n == NB - 1 and g >= NG - 2) or NG * n + g < PAIR_FROM
+            alone = NG * n + g < PAIR_FROM
             if last_unit:
                 if t == 1:
                     nc.sync.dma_start(out=y_dst[:, :, 0 : 2 * D], in_=y[:, :, 0:2, :].rearrange("p h t d -> p h (t d)"))

@@ -22,10 +22,13 @@ NB = 4
 HB = 4
 D = 128
 
-VMODE = ((0, 0), (0, 1), (0, 2), (2, 0), (3, 3))
-TMODE = ((1, 1), (2, 3))
-T_ACC_LAG = 8
-T_BACK_LAG = 11
+VMODE = ((0, 0), (0, 1), (1, 1), (2, 1), (3, 3))
+TMODE = ((1, 0), (2, 3))
+LATE_W = (2, 3)
+W_AT = (22, 24, 38, 40)
+Q_LAG = 2
+T_ACC_LAG = 6
+T_BACK_LAG = 9
 PAIR_FROM = 6
 SPLIT_BLOCK = 9
 FLUSH_LAG = 2
@@ -109,6 +112,28 @@ def tile_chunkedattention_pb_kernel(tc, hidden_states, wk, bk, wv, bv, out_0, ou
         all_codes = {}
         all_scales = {}
 
+        q_wait = []
+        g_wait = []
+
+        def quantize_whole(unit):
+            nc.vector.quantize_mx(out=all_codes[unit][:].bitcast(FP8X4), scales=all_scales[unit][:], in_=grps[unit][:])
+
+        def q_steps():
+            for item in list(q_wait):
+                item[1] -= 1
+                if item[1] == 0:
+                    quantize_whole(item[0])
+                    gate = spool.tile([P, 8], U32, name="gate")
+                    nc.gpsimd.tensor_copy(out=gate[:], in_=all_codes[item[0]][:, 0:8])
+                    q_wait.remove(item)
+                    state["hold"] = False
+
+        def g_steps():
+            if not state["hold"]:
+                for f in g_wait:
+                    f()
+                g_wait.clear()
+
         def transpose_unit(unit, first, last):
             kind, idx = unit
             if first == 0:
@@ -138,7 +163,11 @@ def tile_chunkedattention_pb_kernel(tc, hidden_states, wk, bk, wv, bv, out_0, ou
                 nc.scalar.copy(out=dst, in_=tp[:].rearrange("p (c u) r -> p c r u", c=2))
                 if idx > 0:
                     if s == 3:
-                        nc.vector.quantize_mx(out=all_codes[unit][:].bitcast(FP8X4), scales=all_scales[unit][:], in_=grp[:])
+                        if kind == "w" and idx in LATE_W:
+                            q_wait.append([unit, Q_LAG])
+                            state["hold"] = True
+                        else:
+                            quantize_whole(unit)
                 elif s % 2 == 1:
                     h = s // 2
                     if kind == "w":
@@ -156,7 +185,7 @@ def tile_chunkedattention_pb_kernel(tc, hidden_states, wk, bk, wv, bv, out_0, ou
                             in_=grp[:, 2048 * h : 2048 * (h + 1)],
                         )
 
-        state = {"y": None, "chain": None, "u": None, "seq": 0, "banks": 0, "late": False}
+        state = {"y": None, "chain": None, "u": None, "seq": 0, "banks": 0, "late": False, "hold": False}
         means = {}
         parts = {}
         pending_scales = []
@@ -212,6 +241,15 @@ def tile_chunkedattention_pb_kernel(tc, hidden_states, wk, bk, wv, bv, out_0, ou
                     )
                     pending_scales.remove(item)
                     part_done(n, g)
+
+        firsts = {}
+
+        def g_rest(y, n, g):
+            two = spool.tile([P, HB, 2, D], F32, name="pair_a")
+            nc.gpsimd.tensor_tensor(out=two[:], in0=y[:, :, 0:4:2, :], in1=y[:, :, 1:4:2, :], op=ADD)
+            r = spool.tile([P, 512], F32, name="total", bufs=5)
+            nc.gpsimd.tensor_tensor(out=r[:].rearrange("p (h d) -> p h d", h=HB), in0=two[:, :, 0, :], in1=two[:, :, 1, :], op=ADD)
+            pending_scales.append((r, n, g, state["seq"]))
 
         def bank(n, g, t):
             if n not in means:
@@ -271,33 +309,27 @@ def tile_chunkedattention_pb_kernel(tc, hidden_states, wk, bk, wv, bv, out_0, ou
                 if t == NT - 1:
                     t_acc_wait.append((y, n, g, state["banks"] - 1))
             else:
-                if t == 1:
-                    u = spool.tile([P, HB, D], F32, name="pair_a")
-                    nc.gpsimd.tensor_tensor(out=u[:], in0=y[:, :, 0, :], in1=y[:, :, 1, :], op=ADD)
-                    state["u"] = u
                 if t == 3:
-                    w2 = spool.tile([P, HB, D], F32, name="pair_b")
-                    nc.gpsimd.tensor_tensor(out=w2[:], in0=y[:, :, 2, :], in1=y[:, :, 3, :], op=ADD)
-                    r = spool.tile([P, 512], F32, name="total", bufs=5)
-                    nc.gpsimd.tensor_tensor(
-                        out=r[:].rearrange("p (h d) -> p h d", h=HB), in0=state["u"][:], in1=w2[:], op=ADD
-                    )
-                    pending_scales.append((r, n, g, state["seq"]))
+                    g_wait.append(lambda: g_rest(y, n, g))
 
         banks = [(n, g, t) for n in range(NB) for g in range(NG) for t in range(NT)]
         program = [("T", ("w", 0, 0, 4)), ("B", 0), ("T", ("x", 0, 0, 4))]
-        later = (("x", 1), ("x", 2), ("x", 3), ("w", 1), ("w", 2), ("w", 3))
+        later = (("x", 1), ("x", 2), ("x", 3), ("w", 1))
         for i in range(len(later)):
             program.append(("M", 1))
             program.append(("T", (later[i][0], later[i][1], 0, 2)))
             program.append(("M", 1))
             program.append(("T", (later[i][0], later[i][1], 2, 4)))
-        program.append(("M", 52))
+        done = 8
+        for i in range(4):
+            program.append(("M", W_AT[i] - done))
+            program.append(("T", ("w", 2 + i // 2, 2 * (i % 2), 2 * (i % 2) + 2)))
+            done = W_AT[i]
+        program.append(("M", 64 - done))
         pos = 0
         for kind, arg in program:
             if kind == "T":
                 transpose_unit((arg[0], arg[1]), arg[2], arg[3])
-                flush_scales(state["seq"])
                 if arg == ("w", 3, 2, 4):
                     state["late"] = True
             elif kind == "B":
@@ -306,12 +338,13 @@ def tile_chunkedattention_pb_kernel(tc, hidden_states, wk, bk, wv, bv, out_0, ou
                 for i in range(arg):
                     b = banks[pos + i]
                     bank(b[0], b[1], b[2])
+                    q_steps()
+                    g_steps()
                     t_steps(pos + i)
                     if b[2] == NT - 1:
-                        if state["late"]:
-                            flush_scales(state["seq"] - FLUSH_LAG)
-                        elif arg - 1 - i >= FLUSH_GUARD:
-                            flush_scales(state["seq"] - FLUSH_LAG)
+                        flush_scales(state["seq"] - FLUSH_LAG)
                         state["seq"] += 1
                 pos += arg
         flush_scales(state["seq"])
+        t_steps(1000)
+        t_steps(1000)

@@ -29,7 +29,7 @@ W_AT = (22, 24, 38, 40)
 Q_LAG = 2
 T_ACC_LAG = 6
 T_BACK_LAG = 9
-PAIR_FROM = 6
+PAIR_FROM = 16
 SPLIT_BLOCK = 9
 FLUSH_LAG = 2
 FLUSH_GUARD = 6

@@ -33,6 +33,8 @@ PAIR_FROM = 16
 SPLIT_BLOCK = 9
 FLUSH_LAG = 2
 FLUSH_GUARD = 6
+ON_SCALAR = ((0, 3), (1, 2), (2, 0), (2, 2), (3, 0), (3, 2))
+STORE_LAG = 1
 
 
 def tile_chunkedattention_pb_kernel(tc, hidden_states, wk, bk, wv, bv, out_0, out_1, out_2, out_3):
@@ -251,6 +253,15 @@ def tile_chunkedattention_pb_kernel(tc, hidden_states, wk, bk, wv, bv, out_0, ou
             nc.gpsimd.tensor_tensor(out=r[:].rearrange("p (h d) -> p h d", h=HB), in0=two[:, :, 0, :], in1=two[:, :, 1, :], op=ADD)
             pending_scales.append((r, n, g, state["seq"]))
 
+        late_stores = []
+
+        def store_steps():
+            for item in list(late_stores):
+                item[0] -= 1
+                if item[0] <= 0:
+                    nc.scalar.dma_start(out=item[1], in_=item[2].rearrange("p h t d -> p h (t d)"))
+                    late_stores.remove(item)
+
         def bank(n, g, t):
             if n not in means:
                 means[n] = mpool.tile([P, HB, NG, D], F32, name="means")
@@ -288,7 +299,10 @@ def tile_chunkedattention_pb_kernel(tc, hidden_states, wk, bk, wv, bv, out_0, ou
                     nc.sync.dma_start(out=y_dst[:, :, D * t : D * (t + 1)], in_=y[:, :, t, :])
             elif alone:
                 if t == NT - 1:
-                    nc.sync.dma_start(out=y_dst, in_=y.rearrange("p h t d -> p h (t d)"))
+                    if (n, g) in ON_SCALAR:
+                        late_stores.append([STORE_LAG, y_dst, y])
+                    else:
+                        nc.sync.dma_start(out=y_dst, in_=y.rearrange("p h t d -> p h (t d)"))
             elif t == NT - 1 and g % 2 == 1:
                 nc.sync.dma_start(
                     out=pair_views[n // 2][:, g // 2, HB * (n % 2) : HB * (n % 2 + 1), :],
@@ -338,6 +352,7 @@ def tile_chunkedattention_pb_kernel(tc, hidden_states, wk, bk, wv, bv, out_0, ou
                 for i in range(arg):
                     b = banks[pos + i]
                     bank(b[0], b[1], b[2])
+                    store_steps()
                     q_steps()
                     g_steps()
                     t_steps(pos + i)
@@ -345,6 +360,8 @@ def tile_chunkedattention_pb_kernel(tc, hidden_states, wk, bk, wv, bv, out_0, ou
                         flush_scales(state["seq"] - FLUSH_LAG)
                         state["seq"] += 1
                 pos += arg
+        for i in range(STORE_LAG):
+            store_steps()
         flush_scales(state["seq"])
         t_steps(1000)
         t_steps(1000)

@@ -35,6 +35,7 @@ FLUSH_LAG = 2
 FLUSH_GUARD = 6
 ON_SCALAR = ((0, 3), (1, 2), (2, 0), (2, 2), (3, 0), (3, 2))
 STORE_LAG = 1
+SORTED = (("w", 2), ("w", 3))
 
 
 def tile_chunkedattention_pb_kernel(tc, hidden_states, wk, bk, wv, bv, out_0, out_1, out_2, out_3):
@@ -136,6 +137,23 @@ def tile_chunkedattention_pb_kernel(tc, hidden_states, wk, bk, wv, bv, out_0, ou
                     f()
                 g_wait.clear()
 
+        sorted_words = {}
+
+        def sort_unit(unit, first, last):
+            if unit not in sorted_words:
+                if state["sorted_free"] is None:
+                    two = big.tile([P, 8, E // 2], F32, name="big")
+                    sorted_words[unit] = two[:, 0:4, :]
+                    state["sorted_free"] = two[:, 4:8, :]
+                else:
+                    sorted_words[unit] = state["sorted_free"]
+                    state["sorted_free"] = None
+            src = raw[unit][0][:, raw[unit][1] + first : raw[unit][1] + last, :].bitcast(F32)
+            nc.scalar.copy(
+                out=sorted_words[unit][:, first:last, :].rearrange("p s (c u j) -> p (s c) u j", c=2, u=2),
+                in_=src.rearrange("p s (c j u) -> p (s c) u j", c=2, u=2),
+            )
+
         def transpose_unit(unit, first, last):
             kind, idx = unit
             if first == 0:
@@ -150,11 +168,15 @@ def tile_chunkedattention_pb_kernel(tc, hidden_states, wk, bk, wv, bv, out_0, ou
             grp = grps[unit]
             gwords = grp[:].bitcast(F32)
             for s in range(first, last):
-                words = raw[unit][0][:, raw[unit][1] + s, :].bitcast(F32)
                 tp = tpsum.tile([P, 4, P], F32, name="tp")
-                for c in range(2):
-                    for u in range(2):
-                        nc.tensor.transpose(tp[:, 2 * c + u, :], words[:, 256 * c + u : 256 * (c + 1) : 2], ident[:])
+                if unit in SORTED:
+                    for q in range(4):
+                        nc.tensor.transpose(tp[:, q, :], sorted_words[unit][:, s, P * q : P * (q + 1)], ident[:])
+                else:
+                    words = raw[unit][0][:, raw[unit][1] + s, :].bitcast(F32)
+                    for c in range(2):
+                        for u in range(2):
+                            nc.tensor.transpose(tp[:, 2 * c + u, :], words[:, 256 * c + u : 256 * (c + 1) : 2], ident[:])
                 if unit in (("w", 0), ("x", 0)) and s % 2 == 1:
                     dummy_matmul()
                     dummy_matmul()
@@ -187,7 +209,7 @@ def tile_chunkedattention_pb_kernel(tc, hidden_states, wk, bk, wv, bv, out_0, ou
                             in_=grp[:, 2048 * h : 2048 * (h + 1)],
                         )
 
-        state = {"y": None, "chain": None, "u": None, "seq": 0, "banks": 0, "late": False, "hold": False}
+        state = {"y": None, "chain": None, "u": None, "seq": 0, "banks": 0, "late": False, "hold": False, "sorted_free": None}
         means = {}
         parts = {}
         pending_scales = []
@@ -334,6 +356,8 @@ def tile_chunkedattention_pb_kernel(tc, hidden_states, wk, bk, wv, bv, out_0, ou
             program.append(("T", (later[i][0], later[i][1], 0, 2)))
             program.append(("M", 1))
             program.append(("T", (later[i][0], later[i][1], 2, 4)))
+        program.append(("S", ("w", 2)))
+        program.append(("S", ("w", 3)))
         done = 8
         for i in range(4):
             program.append(("M", W_AT[i] - done))
@@ -348,6 +372,9 @@ def tile_chunkedattention_pb_kernel(tc, hidden_states, wk, bk, wv, bv, out_0, ou
                     state["late"] = True
             elif kind == "B":
                 bias_block(arg)
+            elif kind == "S":
+                sort_unit(arg, 0, 2)
+                sort_unit(arg, 2, 4)
             else:
                 for i in range(arg):
                     b = banks[pos + i]

@@ -177,8 +177,7 @@ def tile_chunkedattention_pb_kernel(tc, hidden_states, wk, bk, wv, bv, out_0, ou
                     for c in range(2):
                         for u in range(2):
                             nc.tensor.transpose(tp[:, 2 * c + u, :], words[:, 256 * c + u : 256 * (c + 1) : 2], ident[:])
-                if unit in (("w", 0), ("x", 0)) and s % 2 == 1:
-                    dummy_matmul()
+                if unit in (("w", 0), ("x", 0)) and s == 1:
                     dummy_matmul()
                 if kind == "w":
                     dst = gwords.rearrange("p (c f u) -> p c f u", c=2, u=2)[:, :, P * s : P * (s + 1), :]
@@ -192,6 +191,12 @@ def tile_chunkedattention_pb_kernel(tc, hidden_states, wk, bk, wv, bv, out_0, ou
                             state["hold"] = True
                         else:
                             quantize_whole(unit)
+                elif kind == "x":
+                    nc.vector.quantize_mx(
+                        out=all_codes[unit][:, 256 * s : 256 * (s + 1)].bitcast(FP8X4),
+                        scales=all_scales[unit][:, 256 * s : 256 * (s + 1)],
+                        in_=grp[:, 1024 * s : 1024 * (s + 1)],
+                    )
                 elif s % 2 == 1:
                     h = s // 2
                     if kind == "w":

@@ -23,6 +23,7 @@ HB = 4
 D = 128
 
 VMODE = ((0, 0), (0, 1), (1, 1), (2, 1), (3, 3))
+SMODE = ((3, 2),)
 TMODE = ((1, 0), (2, 3))
 LATE_W = (2, 3)
 W_AT = (22, 24, 38, 40)
@@ -281,6 +282,19 @@ def tile_chunkedattention_pb_kernel(tc, hidden_states, wk, bk, wv, bv, out_0, ou
             pending_scales.append((r, n, g, state["seq"]))
 
         late_stores = []
+        s_wait = []
+
+        def s_sums():
+            twos = []
+            for y, n, g in s_wait:
+                two = spool.tile([P, HB, 2, D], F32, name="pair_a")
+                nc.vector.tensor_tensor(out=two[:], in0=y[:, :, 0:4:2, :], in1=y[:, :, 1:4:2, :], op=ADD)
+                twos.append(two)
+            for i in range(len(s_wait)):
+                y, n, g = s_wait[i]
+                r = spool.tile([P, 512], F32, name="total", bufs=5)
+                nc.vector.tensor_tensor(out=r[:].rearrange("p (h d) -> p h d", h=HB), in0=twos[i][:, :, 0, :], in1=twos[i][:, :, 1, :], op=ADD)
+                pending_scales.append((r, n, g, state["seq"]))
 
         def store_steps():
             for item in list(late_stores):
@@ -346,6 +360,9 @@ def tile_chunkedattention_pb_kernel(tc, hidden_states, wk, bk, wv, bv, out_0, ou
                         out=m[:, :, g, :], in0=acc3, scalar=0.25, in1=prev.rearrange("p (h d) -> p h d", h=HB), op0=MULT, op1=ADD
                     )
                     part_done(n, g)
+            elif (n, g) in SMODE:
+                if t == NT - 1:
+                    s_wait.append((y, n, g))
             elif (n, g) in TMODE:
                 if t == NT - 1:
                     t_acc_wait.append((y, n, g, state["banks"] - 1))
@@ -394,6 +411,7 @@ def tile_chunkedattention_pb_kernel(tc, hidden_states, wk, bk, wv, bv, out_0, ou
                 pos += arg
         for i in range(STORE_LAG):
             store_steps()
+        s_sums()
         flush_scales(state["seq"])
         t_steps(1000)
         t_steps(1000)

@@ -22,15 +22,15 @@ NB = 4
 HB = 4
 D = 128
 
-VMODE = ((0, 0), (0, 1), (1, 1), (2, 1), (3, 3))
-SMODE = ((3, 2),)
+VMODE = ((0, 0), (0, 1), (1, 1), (2, 1))
+SMODE = ((3, 2), (3, 3))
 TMODE = ((1, 0), (2, 3))
 LATE_W = (2, 3)
 W_AT = (22, 24, 38, 40)
 Q_LAG = 2
 T_ACC_LAG = 6
 T_BACK_LAG = 9
-PAIR_FROM = 16
+PAIR_FROM = 14
 SPLIT_BLOCK = 9
 FLUSH_LAG = 2
 FLUSH_GUARD = 6

@@ -178,7 +178,7 @@ def tile_chunkedattention_pb_kernel(tc, hidden_states, wk, bk, wv, bv, out_0, ou
                     for c in range(2):
                         for u in range(2):
                             nc.tensor.transpose(tp[:, 2 * c + u, :], words[:, 256 * c + u : 256 * (c + 1) : 2], ident[:])
-                if unit in (("w", 0), ("x", 0)) and s == 1:
+                if unit in (("w", 0), ("x", 0)) and s % 2 == 1:
                     dummy_matmul()
                 if kind == "w":
                     dst = gwords.rearrange("p (c f u) -> p c f u", c=2, u=2)[:, :, P * s : P * (s + 1), :]

@@ -155,6 +155,14 @@ def tile_chunkedattention_pb_kernel(tc, hidden_states, wk, bk, wv, bv, out_0, ou
                 in_=src.rearrange("p s (c j u) -> p (s c) u j", c=2, u=2),
             )
 
+        def quantize_w0(c, h):
+            lo = 2048 * c + 1024 * h
+            nc.vector.quantize_mx(
+                out=wc[(0, c)][:, 256 * h : 256 * (h + 1)].bitcast(FP8X4),
+                scales=ws[(0, c)][:, 256 * h : 256 * (h + 1)],
+                in_=grps[("w", 0)][:, lo : lo + 1024],
+            )
+
         def transpose_unit(unit, first, last):
             kind, idx = unit
             if first == 0:
@@ -198,16 +206,15 @@ def tile_chunkedattention_pb_kernel(tc, hidden_states, wk, bk, wv, bv, out_0, ou
                         scales=all_scales[unit][:, 256 * s : 256 * (s + 1)],
                         in_=grp[:, 1024 * s : 1024 * (s + 1)],
                     )
+                    if s == 0:
+                        quantize_w0(1, 1)
                 elif s % 2 == 1:
                     h = s // 2
                     if kind == "w":
                         for c in range(2):
-                            lo = 2048 * c + 1024 * h
-                            nc.vector.quantize_mx(
-                                out=wc[(idx, c)][:, 256 * h : 256 * (h + 1)].bitcast(FP8X4),
-                                scales=ws[(idx, c)][:, 256 * h : 256 * (h + 1)],
-                                in_=grp[:, lo : lo + 1024],
-                            )
+                            if h == 1 and c == 1:
+                                continue
+                            quantize_w0(c, h)
                     else:
                         nc.vector.quantize_mx(
                             out=xc[(idx, h)].bitcast(FP8X4),
@@ -371,7 +378,7 @@ def tile_chunkedattention_pb_kernel(tc, hidden_states, wk, bk, wv, bv, out_0, ou
                     g_wait.append(lambda: g_rest(y, n, g))
 
         banks = [(n, g, t) for n in range(NB) for g in range(NG) for t in range(NT)]
-        program = [("T", ("w", 0, 0, 4)), ("B", 0), ("T", ("x", 0, 0, 4))]
+        program = [("T", ("w", 0, 0, 4)), ("T", ("x", 0, 0, 2)), ("B", 0), ("T", ("x", 0, 2, 4))]
         later = (("x", 1), ("x", 2), ("x", 3), ("w", 1))
         for i in range(len(later)):
             program.append(("M", 1))

@@ -26,6 +26,7 @@ VMODE = ((0, 0), (0, 1), (1, 1), (2, 1))
 SMODE = ((3, 2), (3, 3))
 TMODE = ((1, 0), (2, 3))
 LATE_W = (2, 3)
+RUN_AT = (1, 2, 3, 4, 6, 8, 10, 11)
 W_AT = (22, 24, 38, 40)
 Q_LAG = 2
 T_ACC_LAG = 6
@@ -380,14 +381,14 @@ def tile_chunkedattention_pb_kernel(tc, hidden_states, wk, bk, wv, bv, out_0, ou
         banks = [(n, g, t) for n in range(NB) for g in range(NG) for t in range(NT)]
         program = [("T", ("w", 0, 0, 4)), ("T", ("x", 0, 0, 2)), ("B", 0), ("T", ("x", 0, 2, 4))]
         later = (("x", 1), ("x", 2), ("x", 3), ("w", 1))
+        done = 0
         for i in range(len(later)):
-            program.append(("M", 1))
-            program.append(("T", (later[i][0], later[i][1], 0, 2)))
-            program.append(("M", 1))
-            program.append(("T", (later[i][0], later[i][1], 2, 4)))
+            for half in range(2):
+                program.append(("M", RUN_AT[2 * i + half] - done))
+                program.append(("T", (later[i][0], later[i][1], 2 * half, 2 * half + 2)))
+                done = RUN_AT[2 * i + half]
         program.append(("S", ("w", 2)))
         program.append(("S", ("w", 3)))
-        done = 8
         for i in range(4):
             program.append(("M", W_AT[i] - done))
             program.append(("T", ("w", 2 + i // 2, 2 * (i % 2), 2 * (i % 2) + 2)))

from contextlib import ExitStack

import concourse.mybir as mybir
from concourse.masks import make_identity

FLOPS = 2 * 2048 * 1024 * 2048

F32 = mybir.dt.float32
BF16 = mybir.dt.bfloat16
U32 = mybir.dt.uint32
U8 = mybir.dt.uint8
FP8X4 = mybir.dt.float8_e5m2_x4
ADD = mybir.AluOpType.add
MULT = mybir.AluOpType.mult
COPY = mybir.ActivationFunctionType.Copy

P = 128
E = 1024
NG = 4
NT = 4
NB = 4
HB = 4
D = 128

VMODE = ((0, 0), (0, 1), (1, 1), (2, 1))
SMODE = ((3, 2), (3, 3))
TMODE = ((1, 0), (2, 3))
LATE_W = (2, 3)
RUN_AT = (1, 2, 3, 4, 6, 8, 10, 11)
W_AT = (22, 24, 38, 40)
Q_LAG = 2
T_ACC_LAG = 6
T_BACK_LAG = 9
PAIR_FROM = 14
SPLIT_BLOCK = 9
FLUSH_LAG = 2
FLUSH_GUARD = 6
ON_SCALAR = ((0, 3), (1, 2), (2, 0), (2, 2), (3, 0), (3, 2))
STORE_LAG = 1
SORTED = (("w", 2), ("w", 3))


def tile_chunkedattention_pb_kernel(tc, hidden_states, wk, bk, wv, bv, out_0, out_1, out_2, out_3):
    nc = tc.nc

    x_view = hidden_states.flatten_outer_dims().rearrange("(p g t) k -> p g t k", g=NG, t=NT)
    w_views = []
    for n in range(NB):
        w = (wk, wv)[n // 2]
        w_views.append(w[512 * (n % 2) : 512 * (n % 2 + 1), :].rearrange("(j p) k -> p j k", p=P))
    y_views = [o.rearrange("b h (p g) t d -> p g (b h) (t d)", g=NG) for o in (out_0, out_1)]
    pair_views = [o.rearrange("b h (p q e) t d -> p q (b h) (e t d)", q=NG // 2, e=2) for o in (out_0, out_1)]
    m_views = [o.rearrange("b h (p g) d -> p (b h) (g d)", g=NG) for o in (out_2, out_3)]

    with ExitStack() as ctx:
        const = ctx.enter_context(tc.tile_pool(name="const", bufs=1))
        big = ctx.enter_context(tc.tile_pool(name="big", bufs=7))
        codes = ctx.enter_context(tc.tile_pool(name="codes", bufs=1))
        stage = ctx.enter_context(tc.tile_pool(name="stage", bufs=3))
        spool = ctx.enter_context(tc.tile_pool(name="spool", bufs=2))
        mpool = ctx.enter_context(tc.tile_pool(name="mpool", bufs=2))
        tpsum = ctx.enter_context(tc.psum_pool(name="tpsum", bufs=4))
        apsum = ctx.enter_context(tc.psum_pool(name="apsum", bufs=4))
        ctx.enter_context(tc.manual_schedule())

        ones = const.tile([P, P], BF16, name="ones")
        nc.vector.memset(ones[:], 1.0)
        dummy_rhs = const.tile([P, 512], BF16, name="dummy_rhs")
        nc.vector.memset(dummy_rhs[:], 1.0)
        bias_late = const.tile([P, 2 * E], BF16, name="bias_late")
        bias_rows = const.tile([P, 512], BF16, name="bias_rows")
        nc.vector.memset(bias_rows[:], 0.0)
        warm = const.tile([P, 1], F32, name="warm")
        nc.scalar.activation(out=warm[:], in_=ones[:, 0:1], func=COPY, scale=0.25)
        ident = const.tile([P, P], F32, name="ident")
        make_identity(nc, ident[:])
        bias = const.tile([P, 512], F32, name="bias")
        dummy_out = apsum.tile([P, 512], F32, name="acc")

        def dummy_matmul():
            nc.tensor.matmul(out=dummy_out[:], lhsT=ones[:], rhs=dummy_rhs[:], start=True, stop=True)

        for i in range(4):
            dummy_matmul()

        units = (("w", 0), ("x", 0), ("x", 1), ("x", 2), ("x", 3), ("w", 1), ("w", 2), ("w", 3))
        pieces = {("w", 0): 4, ("x", 0): 4, ("x", 1): 2}
        raw = {}
        for number, unit in enumerate(units):
            src = w_views[unit[1]] if unit[0] == "w" else x_view[:, unit[1], :, :]
            if number % 2 == 0:
                two_units = big.tile([P, 8, E], BF16, name="big")
            base = 4 * (number % 2)
            raw[unit] = (two_units, base)
            n_dma = pieces.get(unit, 1)
            step = 4 // n_dma
            for i in range(n_dma):
                nc.sync.dma_start(
                    out=two_units[:, base + i * step : base + (i + 1) * step, :], in_=src[:, i * step : (i + 1) * step, :]
                )
            if unit == ("w", 0):
                nc.sync.dma_start(out=bias_rows[0:1, 0:512], in_=bk[0:512].rearrange("(o f) -> o f", o=1))
        nc.sync.dma_start(out=bias_late[:, 512:E], in_=bk[512:E].partition_broadcast(P))
        nc.sync.dma_start(out=bias_late[:, E : 2 * E], in_=bv.partition_broadcast(P))

        def bias_block(n):
            bp = apsum.tile([P, 512], F32, name="acc")
            nc.tensor.matmul(out=bp[:], lhsT=ones[:], rhs=bias_rows[:, 512 * n : 512 * (n + 1)], start=True, stop=True)
            nc.scalar.copy(out=bias[:, 512 * n : 512 * (n + 1)], in_=bp[:])

        xc = {}
        xs = {}
        wc = {}
        ws = {}

        grps = {}
        all_codes = {}
        all_scales = {}

        q_wait = []
        g_wait = []

        def quantize_whole(unit):
            nc.vector.quantize_mx(out=all_codes[unit][:].bitcast(FP8X4), scales=all_scales[unit][:], in_=grps[unit][:])

        def q_steps():
            for item in list(q_wait):
                item[1] -= 1
                if item[1] == 0:
                    quantize_whole(item[0])
                    gate = spool.tile([P, 8], U32, name="gate")
                    nc.gpsimd.tensor_copy(out=gate[:], in_=all_codes[item[0]][:, 0:8])
                    q_wait.remove(item)
                    state["hold"] = False

        def g_steps():
            if not state["hold"]:
                for f in g_wait:
                    f()
                g_wait.clear()

        sorted_words = {}

        def sort_unit(unit, first, last):
            if unit not in sorted_words:
                if state["sorted_free"] is None:
                    two = big.tile([P, 8, E // 2], F32, name="big")
                    sorted_words[unit] = two[:, 0:4, :]
                    state["sorted_free"] = two[:, 4:8, :]
                else:
                    sorted_words[unit] = state["sorted_free"]
                    state["sorted_free"] = None
            src = raw[unit][0][:, raw[unit][1] + first : raw[unit][1] + last, :].bitcast(F32)
            nc.scalar.copy(
                out=sorted_words[unit][:, first:last, :].rearrange("p s (c u j) -> p (s c) u j", c=2, u=2),
                in_=src.rearrange("p s (c j u) -> p (s c) u j", c=2, u=2),
            )

        def quantize_w0(c, h):
            lo = 2048 * c + 1024 * h
            nc.vector.quantize_mx(
                out=wc[(0, c)][:, 256 * h : 256 * (h + 1)].bitcast(FP8X4),
                scales=ws[(0, c)][:, 256 * h : 256 * (h + 1)],
                in_=grps[("w", 0)][:, lo : lo + 1024],
            )

        def transpose_unit(unit, first, last):
            kind, idx = unit
            if first == 0:
                grps[unit] = stage.tile([P, 4096], BF16, name="grp", align_bytes=64)
                all_codes[unit] = codes.tile([P, 1024], U32, name="codes_%s%d" % unit, align_bytes=64)
                all_scales[unit] = codes.tile([P, 1024], U8, name="scales_%s%d" % unit, align_bytes=64)
                code_views = wc if kind == "w" else xc
                scale_views = ws if kind == "w" else xs
                for half in range(2):
                    code_views[(idx, half)] = all_codes[unit][:, 512 * half : 512 * (half + 1)]
                    scale_views[(idx, half)] = all_scales[unit][:, 512 * half : 512 * (half + 1)]
            grp = grps[unit]
            gwords = grp[:].bitcast(F32)
            for s in range(first, last):
                tp = tpsum.tile([P, 4, P], F32, name="tp")
                if unit in SORTED:
                    for q in range(4):
                        nc.tensor.transpose(tp[:, q, :], sorted_words[unit][:, s, P * q : P * (q + 1)], ident[:])
                else:
                    words = raw[unit][0][:, raw[unit][1] + s, :].bitcast(F32)
                    for c in range(2):
                        for u in range(2):
                            nc.tensor.transpose(tp[:, 2 * c + u, :], words[:, 256 * c + u : 256 * (c + 1) : 2], ident[:])
                if unit in (("w", 0), ("x", 0)) and s % 2 == 1:
                    dummy_matmul()
                if kind == "w":
                    dst = gwords.rearrange("p (c f u) -> p c f u", c=2, u=2)[:, :, P * s : P * (s + 1), :]
                else:
                    dst = gwords[:, 512 * s : 512 * (s + 1)].rearrange("p (c r u) -> p c r u", c=2, u=2)
                nc.scalar.copy(out=dst, in_=tp[:].rearrange("p (c u) r -> p c r u", c=2))
                if idx > 0:
                    if s == 3:
                        if kind == "w" and idx in LATE_W:
                            q_wait.append([unit, Q_LAG])
                            state["hold"] = True
                        else:
                            quantize_whole(unit)
                elif kind == "x":
                    nc.vector.quantize_mx(
                        out=all_codes[unit][:, 256 * s : 256 * (s + 1)].bitcast(FP8X4),
                        scales=all_scales[unit][:, 256 * s : 256 * (s + 1)],
                        in_=grp[:, 1024 * s : 1024 * (s + 1)],
                    )
                    if s == 0:
                        quantize_w0(1, 1)
                elif s % 2 == 1:
                    h = s // 2
                    if kind == "w":
                        for c in range(2):
                            if h == 1 and c == 1:
                                continue
                            quantize_w0(c, h)
                    else:
                        nc.vector.quantize_mx(
                            out=xc[(idx, h)].bitcast(FP8X4),
                            scales=xs[(idx, h)],
                            in_=grp[:, 2048 * h : 2048 * (h + 1)],
                        )

        state = {"y": None, "chain": None, "u": None, "seq": 0, "banks": 0, "late": False, "hold": False, "sorted_free": None}
        means = {}
        parts = {}
        pending_scales = []
        t_acc_wait = []
        t_back_wait = []

        def t_accumulate(y, n, g):
            at = tpsum.tile([P, HB, P], F32, name="tp")
            for h in range(HB):
                for t in range(NT):
                    nc.tensor.matmul(
                        out=at[:, h, :], lhsT=y[:, h, t, :], rhs=ident[:], is_transpose=True, start=(t == 0), stop=(t == NT - 1)
                    )
            mt = spool.tile([P, HB, P], F32, name="mean_t")
            nc.scalar.activation(out=mt[:], in_=at[:], func=COPY, scale=0.25)
            return mt

        def t_back(mt, n, g):
            bt = tpsum.tile([P, HB, P], F32, name="tp")
            for h in range(HB):
                nc.tensor.transpose(bt[:, h, :], mt[:, h, :], ident[:])
            nc.scalar.copy(out=means[n][:, :, g, :], in_=bt[:])
            part_done(n, g)

        def t_steps(k):
            for item in list(t_back_wait):
                if k >= item[3] + T_BACK_LAG:
                    t_back(item[0], item[1], item[2])
                    t_back_wait.remove(item)
            for item in list(t_acc_wait):
                if k >= item[3] + T_ACC_LAG:
                    t_back_wait.append((t_accumulate(item[0], item[1], item[2]), item[1], item[2], item[3]))
                    t_acc_wait.remove(item)

        def part_done(n, g):
            parts.setdefault(n, []).append(g)
            m = means[n]
            dst = m_views[n // 2][:, HB * (n % 2) : HB * (n % 2 + 1), :]
            if n == SPLIT_BLOCK:
                if g >= 2:
                    nc.scalar.dma_start(out=dst[:, :, D * g : D * (g + 1)], in_=m[:, :, g, :])
                elif (0 in parts[n]) and (1 in parts[n]):
                    nc.scalar.dma_start(out=dst[:, :, 0 : 2 * D], in_=m[:, :, 0:2, :].rearrange("p h g d -> p h (g d)"))
            elif len(parts[n]) == NG:
                nc.scalar.dma_start(out=dst, in_=m[:].rearrange("p h g d -> p h (g d)"))

        def flush_scales(upto):
            for item in list(pending_scales):
                r, n, g, seq = item
                if seq <= upto:
                    nc.scalar.activation(
                        out=means[n][:, :, g, :], in_=r[:].rearrange("p (h d) -> p h d", h=HB), func=COPY, scale=0.25
                    )
                    pending_scales.remove(item)
                    part_done(n, g)

        firsts = {}

        def g_rest(y, n, g):
            two = spool.tile([P, HB, 2, D], F32, name="pair_a")
            nc.gpsimd.tensor_tensor(out=two[:], in0=y[:, :, 0:4:2, :], in1=y[:, :, 1:4:2, :], op=ADD)
            r = spool.tile([P, 512], F32, name="total", bufs=5)
            nc.gpsimd.tensor_tensor(out=r[:].rearrange("p (h d) -> p h d", h=HB), in0=two[:, :, 0, :], in1=two[:, :, 1, :], op=ADD)
            pending_scales.append((r, n, g, state["seq"]))

        late_stores = []
        s_wait = []

        def s_sums():
            twos = []
            for y, n, g in s_wait:
                two = spool.tile([P, HB, 2, D], F32, name="pair_a")
                nc.vector.tensor_tensor(out=two[:], in0=y[:, :, 0:4:2, :], in1=y[:, :, 1:4:2, :], op=ADD)
                twos.append(two)
            for i in range(len(s_wait)):
                y, n, g = s_wait[i]
                r = spool.tile([P, 512], F32, name="total", bufs=5)
                nc.vector.tensor_tensor(out=r[:].rearrange("p (h d) -> p h d", h=HB), in0=twos[i][:, :, 0, :], in1=twos[i][:, :, 1, :], op=ADD)
                pending_scales.append((r, n, g, state["seq"]))

        def store_steps():
            for item in list(late_stores):
                item[0] -= 1
                if item[0] <= 0:
                    nc.scalar.dma_start(out=item[1], in_=item[2].rearrange("p h t d -> p h (t d)"))
                    late_stores.remove(item)

        def bank(n, g, t):
            if n not in means:
                means[n] = mpool.tile([P, HB, NG, D], F32, name="means")
            if t == 0 and g % 2 == 0:
                state["pair"] = big.tile([P, HB, 2, NT, D], F32, name="big")
            pair = state["pair"]
            y = pair[:, :, g % 2, :, :]
            m = means[n]
            state["banks"] += 1
            if state["late"] and state["banks"] % 2 == 1:
                acc = tpsum.tile([P, 512], F32, name="tp")
            else:
                acc = apsum.tile([P, 512], F32, name="acc")
            for c in range(2):
                lo = 256 * (t % 2) + P * c
                nc.tensor.matmul_mx(
                    out=acc[:],
                    lhsT=xc[(g, t // 2)][:, lo : lo + P].bitcast(FP8X4),
                    lhsT_scale=xs[(g, t // 2)][:, lo : lo + P],
                    rhs=wc[(n, c)].bitcast(FP8X4),
                    rhs_scale=ws[(n, c)],
                    start=(c == 0),
                    stop=(c == 1),
                )
            b_n = bias[:] if n == 0 else bias_late[:, 512 * n : 512 * (n + 1)]
            acc3 = acc[:].rearrange("p (h d) -> p h d", h=HB)
            nc.vector.tensor_tensor(out=y[:, :, t, :], in0=acc3, in1=b_n.rearrange("p (h d) -> p h d", h=HB), op=ADD)
            y_dst = y_views[n // 2][:, g, HB * (n % 2) : HB * (n % 2 + 1), :]
            last_unit = False
            alone = NG * n + g < PAIR_FROM
            if last_unit:
                if t == 1:
                    nc.sync.dma_start(out=y_dst[:, :, 0 : 2 * D], in_=y[:, :, 0:2, :].rearrange("p h t d -> p h (t d)"))
                elif t >= 2:
                    nc.sync.dma_start(out=y_dst[:, :, D * t : D * (t + 1)], in_=y[:, :, t, :])
            elif alone:
                if t == NT - 1:
                    if (n, g) in ON_SCALAR:
                        late_stores.append([STORE_LAG, y_dst, y])
                    else:
                        nc.sync.dma_start(out=y_dst, in_=y.rearrange("p h t d -> p h (t d)"))
            elif t == NT - 1 and g % 2 == 1:
                nc.sync.dma_start(
                    out=pair_views[n // 2][:, g // 2, HB * (n % 2) : HB * (n % 2 + 1), :],
                    in_=pair[:].rearrange("p h e t d -> p h (e t d)"),
                )
            if (n, g) in VMODE:
                prev = b_n if t == 0 else state["chain"][:]
                if t < NT - 1:
                    ch = spool.tile([P, 512], F32, name="chain")
                    nc.vector.scalar_tensor_tensor(out=ch[:], in0=acc[:], scalar=0.25, in1=prev, op0=MULT, op1=ADD)
                    state["chain"] = ch
                else:
                    nc.vector.scalar_tensor_tensor(
                        out=m[:, :, g, :], in0=acc3, scalar=0.25, in1=prev.rearrange("p (h d) -> p h d", h=HB), op0=MULT, op1=ADD
                    )
                    part_done(n, g)
            elif (n, g) in SMODE:
                if t == NT - 1:
                    s_wait.append((y, n, g))
            elif (n, g) in TMODE:
                if t == NT - 1:
                    t_acc_wait.append((y, n, g, state["banks"] - 1))
            else:
                if t == 3:
                    g_wait.append(lambda: g_rest(y, n, g))

        banks = [(n, g, t) for n in range(NB) for g in range(NG) for t in range(NT)]
        program = [("T", ("w", 0, 0, 4)), ("T", ("x", 0, 0, 2)), ("B", 0), ("T", ("x", 0, 2, 4))]
        later = (("x", 1), ("x", 2), ("x", 3), ("w", 1))
        done = 0
        for i in range(len(later)):
            for half in range(2):
                program.append(("M", RUN_AT[2 * i + half] - done))
                program.append(("T", (later[i][0], later[i][1], 2 * half, 2 * half + 2)))
                done = RUN_AT[2 * i + half]
        program.append(("S", ("w", 2)))
        program.append(("S", ("w", 3)))
        for i in range(4):
            program.append(("M", W_AT[i] - done))
            program.append(("T", ("w", 2 + i // 2, 2 * (i % 2), 2 * (i % 2) + 2)))
            done = W_AT[i]
        program.append(("M", 64 - done))
        pos = 0
        for kind, arg in program:
            if kind == "T":
                transpose_unit((arg[0], arg[1]), arg[2], arg[3])
                if arg == ("w", 3, 2, 4):
                    state["late"] = True
            elif kind == "B":
                bias_block(arg)
            elif kind == "S":
                sort_unit(arg, 0, 2)
                sort_unit(arg, 2, 4)
            else:
                for i in range(arg):
                    b = banks[pos + i]
                    bank(b[0], b[1], b[2])
                    store_steps()
                    q_steps()
                    g_steps()
                    t_steps(pos + i)
                    if b[2] == NT - 1:
                        flush_scales(state["seq"] - FLUSH_LAG)
                        state["seq"] += 1
                pos += arg
        for i in range(STORE_LAG):
            store_steps()
        s_sums()
        flush_scales(state["seq"])
        t_steps(1000)
        t_steps(1000)
